import numpy as np
import ml_dtypes


def mxq(x, axis, fmt="e4m3"):
    dtype, down = {"e4m3": (ml_dtypes.float8_e4m3fn, 7), "e5m2": (ml_dtypes.float8_e5m2, 14)}[fmt]
    v = np.moveaxis(np.asarray(x, np.float32).astype(ml_dtypes.bfloat16).astype(np.float64), axis, -1)
    blocks = v.reshape(v.shape[:-1] + (-1, 32))
    amax = np.abs(blocks).max(-1, keepdims=True)
    byte = np.maximum(np.where(amax > 0, np.frexp(amax)[1] - 1 + 127, 0) - down, 1)
    scale = np.exp2(byte - 127.0)
    codes = (blocks / scale).astype(np.float32).astype(dtype).astype(np.float64)
    return np.moveaxis((codes * scale).reshape(v.shape), -1, axis)


WIDE = False


def mx_kscale(k):
    if not WIDE:
        return np.ones(k)
    levels = np.array([10, -10, 5, -5, 0])
    a = np.random.permutation(np.resize(levels, k // 512 * 4)).reshape(k // 512, 4)
    idx = np.arange(k)
    return np.exp2(a[idx // 512, idx % 128 // 32])


BF16 = ml_dtypes.bfloat16


def bf(x):
    return np.asarray(x, np.float32).astype(BF16)


def f64(x):
    return np.asarray(x).astype(np.float64)


E2M1 = np.array([0.0, 0.5, 1.0, 1.5, 2.0, 3.0, 4.0, 6.0, -0.0, -0.5, -1.0, -1.5, -2.0, -3.0, -4.0, -6.0])


def pack_weight(w, fmt):
    k, n = w.shape
    w = f64(bf(w)).reshape(k // 32, 32, n)
    amax = np.abs(w).max(1)
    if fmt == "e4m3":
        byte = np.frexp(amax)[1] - 1 + 127 - 7
    else:
        mant, ex = np.frexp(amax / 6.0)
        byte = np.where(mant > 0.5, ex, ex - 1) + 127
    byte = np.clip(np.where(amax > 0, byte, 1), 1, 254)
    scaled = (w * np.exp2(127.0 - byte)[:, None, :]).reshape(k, n).astype(np.float32)
    by_word = np.ascontiguousarray(scaled.reshape(k // 512, 128, 4, n).transpose(0, 1, 3, 2))
    if fmt == "e4m3":
        words = by_word.astype(ml_dtypes.float8_e4m3fn).view(np.uint8)
    else:
        c = by_word.astype(ml_dtypes.float4_e2m1fn).view(np.uint8) & 0xF
        words = c[..., 0::2] | (c[..., 1::2] << 4)
    return np.ascontiguousarray(words), np.ascontiguousarray(byte.astype(np.uint8).reshape(k // 512, 16, n))


def unpack_weight(words, scales, fmt):
    g, p, n, _ = words.shape
    if fmt == "e4m3":
        vals = np.ascontiguousarray(words).view(ml_dtypes.float8_e4m3fn).astype(np.float64)
    else:
        nib = np.empty((g, p, n, 4), np.uint8)
        nib[..., 0::2] = words & 0xF
        nib[..., 1::2] = words >> 4
        vals = E2M1[nib]
    vals = vals * np.repeat(np.exp2(scales.astype(np.float64) - 127.0), 8, axis=1)[..., None]
    return vals.transpose(0, 1, 3, 2).reshape(g * 512, n)

def pack4(w):
    words, scales = pack_weight(w, "e2m1")
    return words.reshape(words.shape[0], 128, -1), scales


def unpack4(words, scales):
    return unpack_weight(words.reshape(words.shape[0], 128, -1, 2), scales, "e2m1")


B, IN, H = 4096, 512, 512


def sigmoid(v):
    return 1.0 / (1.0 + np.exp(-v))


def setup_inputs():
    s = mx_kscale(IN)
    inp = bf(np.random.standard_normal((B, IN)) * s)
    state = bf(np.random.standard_normal((B, H)))
    c = bf(np.tanh(np.random.standard_normal((B, H))))
    W2_words, W2_scales = pack4(np.random.standard_normal((IN, H)) * 0.7 / np.sqrt(IN) / s[:, None])
    U2_words, U2_scales = pack4(np.random.standard_normal((H, H)) * 0.7 / np.sqrt(H))
    bias_gate = bf(np.random.standard_normal((1, H)) * 0.5)
    return {'input': inp,
            'state': state,
            'c': c,
            'W2_words': W2_words,
            'W2_scales': W2_scales,
            'U2_words': U2_words,
            'U2_scales': U2_scales,
            'bias_gate': bias_gate}


def reference(input, state, c, W2_words, W2_scales, U2_words, U2_scales, bias_gate):
    h = f64(state)
    wComp2 = mxq(f64(input), 1, 'e4m3') @ unpack4(W2_words, W2_scales)
    uComp2 = mxq(h, 1, 'e4m3') @ unpack4(U2_words, U2_scales)
    z = sigmoid(wComp2 + uComp2 + f64(bias_gate))
    return z * h + (1.0 - z) * f64(c)

@@ -1,0 +1,193 @@
+from contextlib import ExitStack
+
+import concourse.mybir as mybir
+from concourse.masks import make_identity
+
+F32 = mybir.dt.float32
+BF16 = mybir.dt.bfloat16
+I32 = mybir.dt.int32
+U32 = mybir.dt.uint32
+U8 = mybir.dt.uint8
+FP8X4 = mybir.dt.float8_e4m3fn_x4
+FP4X4 = mybir.dt.float4_e2m1fn_x4
+ALU = mybir.AluOpType
+ACT = mybir.ActivationFunctionType
+
+P = 128
+PACK = 4
+ROWS = 4096
+FEATURES = P * PACK
+SLOTS = ROWS // P
+GROUP_TILES = 4
+GROUP_ROWS = GROUP_TILES * P
+GROUPS = SLOTS // GROUP_TILES
+HALF_TILES = GROUP_TILES // 2
+CHUNKS = FEATURES // P
+WORDS = FEATURES // 2
+INPUT = 0
+STATE = 1
+
+FLOPS = 2 * 2 * ROWS * FEATURES * FEATURES
+
+
+def tile_grulrcell_pb_t_kernel(
+    tc, inp, state, cand, w2_words, w2_scales, u2_words, u2_scales, bias_gate, out
+):
+    nc = tc.nc
+    by_slot = "(p s) f -> p s f"
+    inp_slots = inp.rearrange(by_slot, s=SLOTS)
+    state_slots = state.rearrange(by_slot, s=SLOTS)
+    cand_slots = cand.rearrange(by_slot, s=SLOTS)
+    out_slots = out.rearrange(by_slot, s=SLOTS)
+
+    with ExitStack() as stack:
+        const = stack.enter_context(tc.tile_pool(name="const", bufs=1))
+        resident = stack.enter_context(tc.tile_pool(name="resident", bufs=GROUPS))
+        grouped_pool = stack.enter_context(tc.tile_pool(name="grouped", bufs=2))
+        mx_pool = stack.enter_context(tc.tile_pool(name="mx", bufs=3))
+        gate_pool = stack.enter_context(tc.tile_pool(name="gate", bufs=2))
+        blend_pool = stack.enter_context(tc.tile_pool(name="blend", bufs=2))
+        turned_pool = stack.enter_context(tc.psum_pool(name="turned", bufs=2))
+        sum_pool = stack.enter_context(tc.psum_pool(name="sums", bufs=3))
+        z_pool = stack.enter_context(tc.psum_pool(name="z", bufs=3))
+        stack.enter_context(tc.manual_schedule())
+
+        weight_words = const.tile([P, 2, 2 * FEATURES], U8, align_bytes=64)
+        weight_planes = const.tile([P, 2, FEATURES], U8, align_bytes=64)
+        bias_rows = const.tile([P, P], BF16)
+        bias_rows_f32 = const.tile([P, P], F32)
+        bias_col = const.tile([P, CHUNKS], F32)
+        ident = const.tile([P, P], F32)
+        table_warmer = const.tile([P, 2], F32)
+
+        nc.vector.memset(weight_planes[:].bitcast(I32), 0)
+        nc.vector.memset(bias_rows[:], 0.0)
+        nc.vector.memset(table_warmer[:], 0.0)
+        nc.scalar.activation(out=table_warmer[:, 1:2], in_=table_warmer[:, 0:1], func=ACT.Sigmoid)
+        make_identity(nc, ident[:])
+
+        inp_tiles, state_tiles, cand_tiles = [], [], []
+
+        def load(tiles, slots, tag, g):
+            t = resident.tile([P, GROUP_TILES, FEATURES], BF16, name=tag, tag=tag)
+            nc.sync.dma_start(out=t[:], in_=slots[:, GROUP_TILES * g : GROUP_TILES * (g + 1), :])
+            tiles.append(t)
+
+        def load_weights():
+            for operand, words, scales in ((INPUT, w2_words, w2_scales), (STATE, u2_words, u2_scales)):
+                nc.sync.dma_start(out=weight_words[:, operand, :].bitcast(I32), in_=words[0].bitcast(I32))
+                for quadrant in range(4):
+                    nc.sync.dma_start(
+                        out=weight_planes[32 * quadrant : 32 * quadrant + 4, operand, :].bitcast(I32),
+                        in_=scales[0, 4 * quadrant : 4 * quadrant + 4, :].bitcast(I32),
+                    )
+
+        nc.sync.dma_start(out=bias_rows[0:CHUNKS, :], in_=bias_gate.rearrange("o (j m) -> (o j) m", j=CHUNKS))
+        for g in range(GROUPS + 1):
+            if g < GROUPS:
+                load(inp_tiles, inp_slots, "inp", g)
+                load(state_tiles, state_slots, "state", g)
+            if g == 0:
+                load_weights()
+            else:
+                load(cand_tiles, cand_slots, "cand", g - 1)
+
+        nc.vector.tensor_copy(out=bias_rows_f32[:], in_=bias_rows[:])
+        bias_turned = turned_pool.tile([P, 2, HALF_TILES * P], F32, name="bias_turned", tag="turned")
+        nc.tensor.transpose(bias_turned[:, 0, 0:P], bias_rows_f32[:], ident[:])
+        nc.vector.tensor_copy(out=bias_col[:], in_=bias_turned[:, 0, 0:CHUNKS])
+
+        grouped_tiles, code_tiles, plane_tiles, gate_tiles, minus_tiles, out_tiles = {}, {}, {}, {}, {}, {}
+
+        def exists(g):
+            return 0 <= g < GROUPS
+
+        def turn_in(operand, g, half):
+            if not exists(g):
+                return
+            if operand == INPUT and half == 0:
+                grouped_tiles[g] = grouped_pool.tile(
+                    [P, 2, GROUP_ROWS, PACK], BF16, name="grouped", tag="grouped", align_bytes=64
+                )
+            source = (inp_tiles, state_tiles)[operand][g]
+            turned = turned_pool.tile([P, 2, HALF_TILES * P], F32, name="turned", tag="turned")
+            for n in range(HALF_TILES):
+                words = source[:, HALF_TILES * half + n, :].bitcast(F32)
+                for u in range(2):
+                    nc.tensor.transpose(turned[:, u, P * n : P * (n + 1)], words[:, u:WORDS:2], ident[:])
+            rows = slice(HALF_TILES * P * half, HALF_TILES * P * (half + 1))
+            nc.scalar.copy(
+                out=grouped_tiles[g][:, operand, rows, :].bitcast(F32),
+                in_=turned[:].rearrange("p u r -> p r u"),
+            )
+
+        def quantise(g):
+            if not exists(g):
+                return
+            code_tiles[g] = mx_pool.tile([P, 2, GROUP_ROWS], U32, name="codes", tag="codes", align_bytes=64)
+            plane_tiles[g] = mx_pool.tile([P, 2, GROUP_ROWS], U8, name="planes", tag="planes", align_bytes=64)
+            nc.vector.quantize_mx(
+                out=code_tiles[g][:].rearrange("p o r -> p (o r)").bitcast(FP8X4),
+                scales=plane_tiles[g][:].rearrange("p o r -> p (o r)"),
+                in_=grouped_tiles[g][:].rearrange("p o r t -> p (o r t)"),
+            )
+
+        def gate(g):
+            if not exists(g):
+                return
+            gate_tiles[g] = gate_pool.tile([P, CHUNKS, GROUP_ROWS], F32, name="gate", tag="gate")
+            for j in range(CHUNKS):
+                sums = sum_pool.tile([P, GROUP_ROWS], F32, name="sums", tag="sums")
+                for operand in (INPUT, STATE):
+                    nc.tensor.matmul_mx(
+                        out=sums[:],
+                        lhsT=weight_words[:, operand, 2 * P * j : 2 * P * (j + 1)].bitcast(FP4X4),
+                        lhsT_scale=weight_planes[:, operand, P * j : P * (j + 1)],
+                        rhs=code_tiles[g][:, operand, :].bitcast(FP8X4),
+                        rhs_scale=plane_tiles[g][:, operand, :],
+                        start=(operand == INPUT),
+                        stop=(operand == STATE),
+                    )
+                nc.scalar.activation(
+                    out=gate_tiles[g][:, j, :], in_=sums[:], func=ACT.Sigmoid, bias=bias_col[:, j : j + 1], scale=1.0
+                )
+
+        def blend_products(g, i):
+            if not exists(g):
+                return
+            if i == 0:
+                out_tiles[g] = resident.tile([P, GROUP_TILES, FEATURES], F32, name="result", tag="result")
+                minus_tiles[g] = blend_pool.tile([P, GROUP_TILES, FEATURES], F32, name="minus", tag="minus")
+            z = z_pool.tile([P, FEATURES], F32, name="z", tag="z")
+            for j in range(CHUNKS):
+                nc.tensor.transpose(z[:, P * j : P * (j + 1)], gate_tiles[g][:, j, P * i : P * (i + 1)], ident[:])
+            nc.vector.tensor_tensor(out=out_tiles[g][:, i, :], in0=z[:], in1=state_tiles[g][:, i, :], op=ALU.mult)
+            nc.vector.scalar_tensor_tensor(
+                out=minus_tiles[g][:, i, :],
+                in0=z[:],
+                scalar=1.0,
+                in1=cand_tiles[g][:, i, :],
+                op0=ALU.subtract,
+                op1=ALU.mult,
+            )
+
+        def blend_difference(g, half):
+            if not exists(g):
+                return
+            tiles = slice(HALF_TILES * half, HALF_TILES * (half + 1))
+            result = out_tiles[g][:, tiles, :]
+            nc.gpsimd.tensor_tensor(out=result, in0=result, in1=minus_tiles[g][:, tiles, :], op=ALU.subtract)
+            first = GROUP_TILES * g + HALF_TILES * half
+            nc.sync.dma_start(out=out_slots[:, first : first + HALF_TILES, :], in_=result)
+
+        for g in range(-3, GROUPS):
+            for n in range(HALF_TILES):
+                blend_products(g, n)
+                turn_in(STATE, g + 2, n)
+            blend_difference(g, 0)
+            quantise(g + 2)
+            gate(g + 1)
+            for n in range(HALF_TILES):
+                blend_products(g, HALF_TILES + n)
+                turn_in(INPUT, g + 3, n)
+            blend_difference(g, 1)

@@ -17,15 +17,20 @@ P = 128
 PACK = 4
 ROWS = 4096
 FEATURES = P * PACK
-SLOTS = ROWS // P
+TILES = ROWS // P
 GROUP_TILES = 4
 GROUP_ROWS = GROUP_TILES * P
-GROUPS = SLOTS // GROUP_TILES
-HALF_TILES = GROUP_TILES // 2
+GROUPS = TILES // GROUP_TILES
 CHUNKS = FEATURES // P
 WORDS = FEATURES // 2
 INPUT = 0
 STATE = 1
+PART_TILES = 2
+GROUP_PARTS = 2 * GROUP_TILES // PART_TILES
+PARTS = GROUPS * GROUP_PARTS
+RUN_CHUNKS = 2
+GATE_RUNS = CHUNKS // RUN_CHUNKS
+TURN_AHEAD = 10
 
 FLOPS = 2 * 2 * ROWS * FEATURES * FEATURES
 
@@ -34,21 +39,21 @@ def tile_grulrcell_pb_t_kernel(
     tc, inp, state, cand, w2_words, w2_scales, u2_words, u2_scales, bias_gate, out
 ):
     nc = tc.nc
-    by_slot = "(p s) f -> p s f"
-    inp_slots = inp.rearrange(by_slot, s=SLOTS)
-    state_slots = state.rearrange(by_slot, s=SLOTS)
-    cand_slots = cand.rearrange(by_slot, s=SLOTS)
-    out_slots = out.rearrange(by_slot, s=SLOTS)
+    by_tile = "(p t) f -> p t f"
+    inp_tiles = inp.rearrange(by_tile, t=TILES)
+    state_tiles = state.rearrange(by_tile, t=TILES)
+    cand_tiles = cand.rearrange(by_tile, t=TILES)
+    out_tiles = out.rearrange(by_tile, t=TILES)
 
     with ExitStack() as stack:
         const = stack.enter_context(tc.tile_pool(name="const", bufs=1))
         resident = stack.enter_context(tc.tile_pool(name="resident", bufs=GROUPS))
-        grouped_pool = stack.enter_context(tc.tile_pool(name="grouped", bufs=2))
-        mx_pool = stack.enter_context(tc.tile_pool(name="mx", bufs=3))
+        mx_pool = stack.enter_context(tc.tile_pool(name="mx", bufs=2))
         gate_pool = stack.enter_context(tc.tile_pool(name="gate", bufs=2))
-        blend_pool = stack.enter_context(tc.tile_pool(name="blend", bufs=2))
-        turned_pool = stack.enter_context(tc.psum_pool(name="turned", bufs=2))
-        sum_pool = stack.enter_context(tc.psum_pool(name="sums", bufs=3))
+        blend_pool = stack.enter_context(tc.tile_pool(name="blend", bufs=6))
+        result_pool = stack.enter_context(tc.tile_pool(name="result", bufs=TILES))
+        turned_pool = stack.enter_context(tc.psum_pool(name="turned", bufs=3))
+        sum_pool = stack.enter_context(tc.psum_pool(name="sums", bufs=RUN_CHUNKS))
         z_pool = stack.enter_context(tc.psum_pool(name="z", bufs=3))
         stack.enter_context(tc.manual_schedule())
 
@@ -66,12 +71,12 @@ def tile_grulrcell_pb_t_kernel(
         nc.scalar.activation(out=table_warmer[:, 1:2], in_=table_warmer[:, 0:1], func=ACT.Sigmoid)
         make_identity(nc, ident[:])
 
-        inp_tiles, state_tiles, cand_tiles = [], [], []
+        inp_groups, state_groups, cand_groups = [], [], []
 
-        def load(tiles, slots, tag, g):
+        def load(groups, dram_tiles, tag, g):
             t = resident.tile([P, GROUP_TILES, FEATURES], BF16, name=tag, tag=tag)
-            nc.sync.dma_start(out=t[:], in_=slots[:, GROUP_TILES * g : GROUP_TILES * (g + 1), :])
-            tiles.append(t)
+            nc.sync.dma_start(out=t[:], in_=dram_tiles[:, GROUP_TILES * g : GROUP_TILES * (g + 1), :])
+            groups.append(t)
 
         def load_weights():
             for operand, words, scales in ((INPUT, w2_words, w2_scales), (STATE, u2_words, u2_scales)):
@@ -83,60 +88,59 @@ def tile_grulrcell_pb_t_kernel(
                     )
 
         nc.sync.dma_start(out=bias_rows[0:CHUNKS, :], in_=bias_gate.rearrange("o (j m) -> (o j) m", j=CHUNKS))
-        for g in range(GROUPS + 1):
+        for g in range(GROUPS + 2):
             if g < GROUPS:
-                load(inp_tiles, inp_slots, "inp", g)
-                load(state_tiles, state_slots, "state", g)
+                load(inp_groups, inp_tiles, "inp", g)
+            if g >= 2:
+                load(cand_groups, cand_tiles, "cand", g - 2)
+            if g < GROUPS:
+                load(state_groups, state_tiles, "state", g)
             if g == 0:
                 load_weights()
-            else:
-                load(cand_tiles, cand_slots, "cand", g - 1)
 
         nc.vector.tensor_copy(out=bias_rows_f32[:], in_=bias_rows[:])
-        bias_turned = turned_pool.tile([P, 2, HALF_TILES * P], F32, name="bias_turned", tag="turned")
+        bias_turned = turned_pool.tile([P, 2, PART_TILES * P], F32, name="bias_turned", tag="turned")
         nc.tensor.transpose(bias_turned[:, 0, 0:P], bias_rows_f32[:], ident[:])
         nc.vector.tensor_copy(out=bias_col[:], in_=bias_turned[:, 0, 0:CHUNKS])
 
-        grouped_tiles, code_tiles, plane_tiles, gate_tiles, minus_tiles, out_tiles = {}, {}, {}, {}, {}, {}
+        grouped_tiles, code_tiles, plane_tiles, gate_tiles = {}, {}, {}, {}
 
-        def exists(g):
-            return 0 <= g < GROUPS
-
-        def turn_in(operand, g, half):
-            if not exists(g):
+        def turn_in(part):
+            if not 0 <= part < PARTS:
                 return
-            if operand == INPUT and half == 0:
-                grouped_tiles[g] = grouped_pool.tile(
+            g, q = divmod(part, GROUP_PARTS)
+            operand, half = divmod(q, 2)
+            if q == 0:
+                grouped_tiles[g] = mx_pool.tile(
                     [P, 2, GROUP_ROWS, PACK], BF16, name="grouped", tag="grouped", align_bytes=64
                 )
-            source = (inp_tiles, state_tiles)[operand][g]
-            turned = turned_pool.tile([P, 2, HALF_TILES * P], F32, name="turned", tag="turned")
-            for n in range(HALF_TILES):
-                words = source[:, HALF_TILES * half + n, :].bitcast(F32)
+            source = (inp_groups, state_groups)[operand][g]
+            turned = turned_pool.tile([P, 2, PART_TILES * P], F32, name="turned", tag="turned")
+            for n in range(PART_TILES):
+                words = source[:, PART_TILES * half + n, :].bitcast(F32)
                 for u in range(2):
                     nc.tensor.transpose(turned[:, u, P * n : P * (n + 1)], words[:, u:WORDS:2], ident[:])
-            rows = slice(HALF_TILES * P * half, HALF_TILES * P * (half + 1))
+            rows = slice(PART_TILES * P * half, PART_TILES * P * (half + 1))
             nc.scalar.copy(
                 out=grouped_tiles[g][:, operand, rows, :].bitcast(F32),
                 in_=turned[:].rearrange("p u r -> p r u"),
             )
 
         def quantise(g):
-            if not exists(g):
-                return
             code_tiles[g] = mx_pool.tile([P, 2, GROUP_ROWS], U32, name="codes", tag="codes", align_bytes=64)
             plane_tiles[g] = mx_pool.tile([P, 2, GROUP_ROWS], U8, name="planes", tag="planes", align_bytes=64)
             nc.vector.quantize_mx(
                 out=code_tiles[g][:].rearrange("p o r -> p (o r)").bitcast(FP8X4),
                 scales=plane_tiles[g][:].rearrange("p o r -> p (o r)"),
-                in_=grouped_tiles[g][:].rearrange("p o r t -> p (o r t)"),
+                in_=grouped_tiles[g][:].rearrange("p o r j -> p (o r j)"),
             )
 
-        def gate(g):
-            if not exists(g):
+        def gate_run(g, run):
+            if not 0 <= g < GROUPS:
                 return
-            gate_tiles[g] = gate_pool.tile([P, CHUNKS, GROUP_ROWS], F32, name="gate", tag="gate")
-            for j in range(CHUNKS):
+            if run == 0:
+                gate_tiles[g] = gate_pool.tile([P, CHUNKS, GROUP_ROWS], F32, name="gate", tag="gate")
+            for j in range(RUN_CHUNKS * run, RUN_CHUNKS * (run + 1)):
                 sums = sum_pool.tile([P, GROUP_ROWS], F32, name="sums", tag="sums")
                 for operand in (INPUT, STATE):
                     nc.tensor.matmul_mx(
@@ -152,42 +156,28 @@ def tile_grulrcell_pb_t_kernel(
                     out=gate_tiles[g][:, j, :], in_=sums[:], func=ACT.Sigmoid, bias=bias_col[:, j : j + 1], scale=1.0
                 )
 
-        def blend_products(g, i):
-            if not exists(g):
+        def blend(t):
+            if t < 0:
                 return
-            if i == 0:
-                out_tiles[g] = resident.tile([P, GROUP_TILES, FEATURES], F32, name="result", tag="result")
-                minus_tiles[g] = blend_pool.tile([P, GROUP_TILES, FEATURES], F32, name="minus", tag="minus")
+            g, i = divmod(t, GROUP_TILES)
             z = z_pool.tile([P, FEATURES], F32, name="z", tag="z")
             for j in range(CHUNKS):
                 nc.tensor.transpose(z[:, P * j : P * (j + 1)], gate_tiles[g][:, j, P * i : P * (i + 1)], ident[:])
-            nc.vector.tensor_tensor(out=out_tiles[g][:, i, :], in0=z[:], in1=state_tiles[g][:, i, :], op=ALU.mult)
+            result = result_pool.tile([P, FEATURES], F32, name="result", tag="result")
+            minus = blend_pool.tile([P, FEATURES], F32, name="minus", tag="minus")
+            nc.vector.tensor_tensor(out=result[:], in0=z[:], in1=state_groups[g][:, i, :], op=ALU.mult)
             nc.vector.scalar_tensor_tensor(
-                out=minus_tiles[g][:, i, :],
-                in0=z[:],
-                scalar=1.0,
-                in1=cand_tiles[g][:, i, :],
-                op0=ALU.subtract,
-                op1=ALU.mult,
+                out=minus[:], in0=z[:], scalar=1.0, in1=cand_groups[g][:, i, :], op0=ALU.subtract, op1=ALU.mult
             )
+            nc.gpsimd.tensor_tensor(out=result[:], in0=result[:], in1=minus[:], op=ALU.subtract)
+            nc.sync.dma_start(out=out_tiles[:, t, :], in_=result[:])
 
-        def blend_difference(g, half):
-            if not exists(g):
-                return
-            tiles = slice(HALF_TILES * half, HALF_TILES * (half + 1))
-            result = out_tiles[g][:, tiles, :]
-            nc.gpsimd.tensor_tensor(out=result, in0=result, in1=minus_tiles[g][:, tiles, :], op=ALU.subtract)
-            first = GROUP_TILES * g + HALF_TILES * half
-            nc.sync.dma_start(out=out_slots[:, first : first + HALF_TILES, :], in_=result)
-
-        for g in range(-3, GROUPS):
-            for n in range(HALF_TILES):
-                blend_products(g, n)
-                turn_in(STATE, g + 2, n)
-            blend_difference(g, 0)
-            quantise(g + 2)
-            gate(g + 1)
-            for n in range(HALF_TILES):
-                blend_products(g, HALF_TILES + n)
-                turn_in(INPUT, g + 3, n)
-            blend_difference(g, 1)
+        for t in range(-TURN_AHEAD, TILES):
+            g, run = divmod(t + GATE_RUNS + 1, GROUP_TILES)
+            if run < GATE_RUNS:
+                gate_run(g, run)
+            blend(t)
+            part = t + TURN_AHEAD
+            turn_in(part)
+            if part < PARTS and part % GROUP_PARTS == GROUP_PARTS - 1:
+                quantise(part // GROUP_PARTS)

@@ -31,6 +31,7 @@ PARTS = GROUPS * GROUP_PARTS
 RUN_CHUNKS = 2
 GATE_RUNS = CHUNKS // RUN_CHUNKS
 TURN_AHEAD = 10
+PAIR = 2
 
 FLOPS = 2 * 2 * ROWS * FEATURES * FEATURES
 
@@ -50,8 +51,8 @@ def tile_grulrcell_pb_t_kernel(
         resident = stack.enter_context(tc.tile_pool(name="resident", bufs=GROUPS))
         mx_pool = stack.enter_context(tc.tile_pool(name="mx", bufs=2))
         gate_pool = stack.enter_context(tc.tile_pool(name="gate", bufs=2))
-        blend_pool = stack.enter_context(tc.tile_pool(name="blend", bufs=6))
-        result_pool = stack.enter_context(tc.tile_pool(name="result", bufs=TILES))
+        blend_pool = stack.enter_context(tc.tile_pool(name="blend", bufs=3))
+        result_pool = stack.enter_context(tc.tile_pool(name="result", bufs=TILES // PAIR))
         turned_pool = stack.enter_context(tc.psum_pool(name="turned", bufs=3))
         sum_pool = stack.enter_context(tc.psum_pool(name="sums", bufs=RUN_CHUNKS))
         z_pool = stack.enter_context(tc.psum_pool(name="z", bufs=3))
@@ -103,7 +104,7 @@ def tile_grulrcell_pb_t_kernel(
         nc.tensor.transpose(bias_turned[:, 0, 0:P], bias_rows_f32[:], ident[:])
         nc.vector.tensor_copy(out=bias_col[:], in_=bias_turned[:, 0, 0:CHUNKS])
 
-        grouped_tiles, code_tiles, plane_tiles, gate_tiles = {}, {}, {}, {}
+        grouped_tiles, code_tiles, plane_tiles, gate_tiles, result_tiles, minus_tiles = {}, {}, {}, {}, {}, {}
 
         def turn_in(part):
             if not 0 <= part < PARTS:
@@ -160,17 +161,21 @@ def tile_grulrcell_pb_t_kernel(
             if t < 0:
                 return
             g, i = divmod(t, GROUP_TILES)
+            pair, n = divmod(t, PAIR)
             z = z_pool.tile([P, FEATURES], F32, name="z", tag="z")
             for j in range(CHUNKS):
                 nc.tensor.transpose(z[:, P * j : P * (j + 1)], gate_tiles[g][:, j, P * i : P * (i + 1)], ident[:])
-            result = result_pool.tile([P, FEATURES], F32, name="result", tag="result")
-            minus = blend_pool.tile([P, FEATURES], F32, name="minus", tag="minus")
-            nc.vector.tensor_tensor(out=result[:], in0=z[:], in1=state_groups[g][:, i, :], op=ALU.mult)
+            if n == 0:
+                result_tiles[pair] = result_pool.tile([P, PAIR, FEATURES], F32, name="result", tag="result")
+                minus_tiles[pair] = blend_pool.tile([P, PAIR, FEATURES], F32, name="minus", tag="minus")
+            result, minus = result_tiles[pair], minus_tiles[pair]
+            nc.vector.tensor_tensor(out=result[:, n, :], in0=z[:], in1=state_groups[g][:, i, :], op=ALU.mult)
             nc.vector.scalar_tensor_tensor(
-                out=minus[:], in0=z[:], scalar=1.0, in1=cand_groups[g][:, i, :], op0=ALU.subtract, op1=ALU.mult
+                out=minus[:, n, :], in0=z[:], scalar=1.0, in1=cand_groups[g][:, i, :], op0=ALU.subtract, op1=ALU.mult
             )
-            nc.gpsimd.tensor_tensor(out=result[:], in0=result[:], in1=minus[:], op=ALU.subtract)
-            nc.sync.dma_start(out=out_tiles[:, t, :], in_=result[:])
+            if n == PAIR - 1:
+                nc.gpsimd.tensor_tensor(out=result[:], in0=result[:], in1=minus[:], op=ALU.subtract)
+                nc.sync.dma_start(out=out_tiles[:, PAIR * pair : PAIR * (pair + 1), :], in_=result[:])
 
         for t in range(-TURN_AHEAD, TILES):
             g, run = divmod(t + GATE_RUNS + 1, GROUP_TILES)

@@ -22,16 +22,18 @@ GROUP_TILES = 4
 GROUP_ROWS = GROUP_TILES * P
 GROUPS = TILES // GROUP_TILES
 CHUNKS = FEATURES // P
+UNITS = GROUPS * CHUNKS
 WORDS = FEATURES // 2
 INPUT = 0
 STATE = 1
 PART_TILES = 2
 GROUP_PARTS = 2 * GROUP_TILES // PART_TILES
 PARTS = GROUPS * GROUP_PARTS
-RUN_CHUNKS = 2
-GATE_RUNS = CHUNKS // RUN_CHUNKS
+HEAD_PARTS = 6
 TURN_AHEAD = 10
-PAIR = 2
+CATCH_UP = 2
+RUN_UNITS = 2
+SPLIT_GROUPS = 2
 
 FLOPS = 2 * 2 * ROWS * FEATURES * FEATURES
 
@@ -49,12 +51,14 @@ def tile_grulrcell_pb_t_kernel(
     with ExitStack() as stack:
         const = stack.enter_context(tc.tile_pool(name="const", bufs=1))
         resident = stack.enter_context(tc.tile_pool(name="resident", bufs=GROUPS))
-        mx_pool = stack.enter_context(tc.tile_pool(name="mx", bufs=2))
-        gate_pool = stack.enter_context(tc.tile_pool(name="gate", bufs=2))
-        blend_pool = stack.enter_context(tc.tile_pool(name="blend", bufs=3))
-        result_pool = stack.enter_context(tc.tile_pool(name="result", bufs=TILES // PAIR))
+        grouped_pool = stack.enter_context(tc.tile_pool(name="grouped", bufs=4))
+        mx_pool = stack.enter_context(tc.tile_pool(name="mx", bufs=6))
+        gate_pool = stack.enter_context(tc.tile_pool(name="gate", bufs=4))
+        blend_pool = stack.enter_context(tc.tile_pool(name="blend", bufs=4))
+        result_pool = stack.enter_context(tc.tile_pool(name="result", bufs=GROUPS - 1))
+        last_pool = stack.enter_context(tc.tile_pool(name="last", bufs=CHUNKS))
         turned_pool = stack.enter_context(tc.psum_pool(name="turned", bufs=3))
-        sum_pool = stack.enter_context(tc.psum_pool(name="sums", bufs=RUN_CHUNKS))
+        sum_pool = stack.enter_context(tc.psum_pool(name="sums", bufs=2))
         z_pool = stack.enter_context(tc.psum_pool(name="z", bufs=3))
         stack.enter_context(tc.manual_schedule())
 
@@ -66,22 +70,30 @@ def tile_grulrcell_pb_t_kernel(
         ident = const.tile([P, P], F32)
         table_warmer = const.tile([P, 2], F32)
 
-        nc.vector.memset(weight_planes[:].bitcast(I32), 0)
         nc.vector.memset(bias_rows[:], 0.0)
+        nc.vector.memset(weight_planes[:].bitcast(I32), 0)
         nc.vector.memset(table_warmer[:], 0.0)
         nc.scalar.activation(out=table_warmer[:, 1:2], in_=table_warmer[:, 0:1], func=ACT.Sigmoid)
         make_identity(nc, ident[:])
 
-        inp_groups, state_groups, cand_groups = [], [], []
+        sources = {}
 
-        def load(groups, dram_tiles, tag, g):
+        def load(dram_tiles, tag, g, pieces):
             t = resident.tile([P, GROUP_TILES, FEATURES], BF16, name=tag, tag=tag)
-            nc.sync.dma_start(out=t[:], in_=dram_tiles[:, GROUP_TILES * g : GROUP_TILES * (g + 1), :])
-            groups.append(t)
+            n = GROUP_TILES // pieces
+            return t, [
+                (t[:, n * i : n * (i + 1), :], dram_tiles[:, GROUP_TILES * g + n * i : GROUP_TILES * g + n * (i + 1), :])
+                for i in range(pieces)
+            ]
+
+        def start(moves):
+            for dst, src in moves:
+                nc.sync.dma_start(out=dst, in_=src)
 
         def load_weights():
-            for operand, words, scales in ((INPUT, w2_words, w2_scales), (STATE, u2_words, u2_scales)):
+            for operand, words in ((INPUT, w2_words), (STATE, u2_words)):
                 nc.sync.dma_start(out=weight_words[:, operand, :].bitcast(I32), in_=words[0].bitcast(I32))
+            for operand, scales in ((INPUT, w2_scales), (STATE, u2_scales)):
                 for quadrant in range(4):
                     nc.sync.dma_start(
                         out=weight_planes[32 * quadrant : 32 * quadrant + 4, operand, :].bitcast(I32),
@@ -89,33 +101,30 @@ def tile_grulrcell_pb_t_kernel(
                     )
 
         nc.sync.dma_start(out=bias_rows[0:CHUNKS, :], in_=bias_gate.rearrange("o (j m) -> (o j) m", j=CHUNKS))
-        for g in range(GROUPS + 2):
-            if g < GROUPS:
-                load(inp_groups, inp_tiles, "inp", g)
-            if g >= 2:
-                load(cand_groups, cand_tiles, "cand", g - 2)
-            if g < GROUPS:
-                load(state_groups, state_tiles, "state", g)
-            if g == 0:
+        for g in range(GROUPS):
+            pieces = 2 if g < SPLIT_GROUPS else 1
+            sources[(INPUT, g)], moves = load(inp_tiles, "inp", g, pieces)
+            start(moves)
+            if g == 1:
                 load_weights()
+            sources[(STATE, g)], moves = load(state_tiles, "state", g, pieces)
+            start(moves)
+            if g >= 1:
+                sources[("c", g - 1)], moves = load(cand_tiles, "cand", g - 1, 1)
+                start(moves)
+        sources[("c", GROUPS - 1)], moves = load(cand_tiles, "cand", GROUPS - 1, 1)
+        start(moves)
 
-        nc.vector.tensor_copy(out=bias_rows_f32[:], in_=bias_rows[:])
-        bias_turned = turned_pool.tile([P, 2, PART_TILES * P], F32, name="bias_turned", tag="turned")
-        nc.tensor.transpose(bias_turned[:, 0, 0:P], bias_rows_f32[:], ident[:])
-        nc.vector.tensor_copy(out=bias_col[:], in_=bias_turned[:, 0, 0:CHUNKS])
-
-        grouped_tiles, code_tiles, plane_tiles, gate_tiles, result_tiles, minus_tiles = {}, {}, {}, {}, {}, {}
+        grouped_tiles, code_tiles, plane_tiles, gate_tiles, z_tiles, result_tiles = {}, {}, {}, {}, {}, {}
 
         def turn_in(part):
-            if not 0 <= part < PARTS:
-                return
             g, q = divmod(part, GROUP_PARTS)
             operand, half = divmod(q, 2)
-            if q == 0:
-                grouped_tiles[g] = mx_pool.tile(
-                    [P, 2, GROUP_ROWS, PACK], BF16, name="grouped", tag="grouped", align_bytes=64
+            if half == 0:
+                grouped_tiles[(g, operand)] = grouped_pool.tile(
+                    [P, GROUP_ROWS, PACK], BF16, name="grouped", tag="grouped", align_bytes=64
                 )
-            source = (inp_groups, state_groups)[operand][g]
+            source = sources[(operand, g)]
             turned = turned_pool.tile([P, 2, PART_TILES * P], F32, name="turned", tag="turned")
             for n in range(PART_TILES):
                 words = source[:, PART_TILES * half + n, :].bitcast(F32)
@@ -123,66 +132,96 @@ def tile_grulrcell_pb_t_kernel(
                     nc.tensor.transpose(turned[:, u, P * n : P * (n + 1)], words[:, u:WORDS:2], ident[:])
             rows = slice(PART_TILES * P * half, PART_TILES * P * (half + 1))
             nc.scalar.copy(
-                out=grouped_tiles[g][:, operand, rows, :].bitcast(F32),
+                out=grouped_tiles[(g, operand)][:, rows, :].bitcast(F32),
                 in_=turned[:].rearrange("p u r -> p r u"),
             )
 
-        def quantise(g):
-            code_tiles[g] = mx_pool.tile([P, 2, GROUP_ROWS], U32, name="codes", tag="codes", align_bytes=64)
-            plane_tiles[g] = mx_pool.tile([P, 2, GROUP_ROWS], U8, name="planes", tag="planes", align_bytes=64)
+        def quantise(g, operand):
+            key = (g, operand)
+            code_tiles[key] = mx_pool.tile([P, GROUP_ROWS], U32, name="codes", tag="codes", align_bytes=64)
+            plane_tiles[key] = mx_pool.tile([P, GROUP_ROWS], U8, name="planes", tag="planes", align_bytes=64)
             nc.vector.quantize_mx(
-                out=code_tiles[g][:].rearrange("p o r -> p (o r)").bitcast(FP8X4),
-                scales=plane_tiles[g][:].rearrange("p o r -> p (o r)"),
-                in_=grouped_tiles[g][:].rearrange("p o r j -> p (o r j)"),
+                out=code_tiles[key][:].bitcast(FP8X4),
+                scales=plane_tiles[key][:],
+                in_=grouped_tiles[key][:].rearrange("p r j -> p (r j)"),
             )
 
-        def gate_run(g, run):
-            if not 0 <= g < GROUPS:
+        def gate(unit):
+            if unit >= UNITS:
                 return
-            if run == 0:
-                gate_tiles[g] = gate_pool.tile([P, CHUNKS, GROUP_ROWS], F32, name="gate", tag="gate")
-            for j in range(RUN_CHUNKS * run, RUN_CHUNKS * (run + 1)):
-                sums = sum_pool.tile([P, GROUP_ROWS], F32, name="sums", tag="sums")
-                for operand in (INPUT, STATE):
-                    nc.tensor.matmul_mx(
-                        out=sums[:],
-                        lhsT=weight_words[:, operand, 2 * P * j : 2 * P * (j + 1)].bitcast(FP4X4),
-                        lhsT_scale=weight_planes[:, operand, P * j : P * (j + 1)],
-                        rhs=code_tiles[g][:, operand, :].bitcast(FP8X4),
-                        rhs_scale=plane_tiles[g][:, operand, :],
-                        start=(operand == INPUT),
-                        stop=(operand == STATE),
-                    )
-                nc.scalar.activation(
-                    out=gate_tiles[g][:, j, :], in_=sums[:], func=ACT.Sigmoid, bias=bias_col[:, j : j + 1], scale=1.0
+            g, j = divmod(unit, CHUNKS)
+            sums = sum_pool.tile([P, GROUP_ROWS], F32, name="sums", tag="sums")
+            for operand in (INPUT, STATE):
+                nc.tensor.matmul_mx(
+                    out=sums[:],
+                    lhsT=weight_words[:, operand, 2 * P * j : 2 * P * (j + 1)].bitcast(FP4X4),
+                    lhsT_scale=weight_planes[:, operand, P * j : P * (j + 1)],
+                    rhs=code_tiles[(g, operand)][:].bitcast(FP8X4),
+                    rhs_scale=plane_tiles[(g, operand)][:],
+                    start=(operand == INPUT),
+                    stop=(operand == STATE),
                 )
-
-        def blend(t):
-            if t < 0:
-                return
-            g, i = divmod(t, GROUP_TILES)
-            pair, n = divmod(t, PAIR)
-            z = z_pool.tile([P, FEATURES], F32, name="z", tag="z")
-            for j in range(CHUNKS):
-                nc.tensor.transpose(z[:, P * j : P * (j + 1)], gate_tiles[g][:, j, P * i : P * (i + 1)], ident[:])
-            if n == 0:
-                result_tiles[pair] = result_pool.tile([P, PAIR, FEATURES], F32, name="result", tag="result")
-                minus_tiles[pair] = blend_pool.tile([P, PAIR, FEATURES], F32, name="minus", tag="minus")
-            result, minus = result_tiles[pair], minus_tiles[pair]
-            nc.vector.tensor_tensor(out=result[:, n, :], in0=z[:], in1=state_groups[g][:, i, :], op=ALU.mult)
-            nc.vector.scalar_tensor_tensor(
-                out=minus[:, n, :], in0=z[:], scalar=1.0, in1=cand_groups[g][:, i, :], op0=ALU.subtract, op1=ALU.mult
+            gate_tiles[unit] = gate_pool.tile([P, GROUP_ROWS], F32, name="gate", tag="gate")
+            nc.scalar.activation(
+                out=gate_tiles[unit][:], in_=sums[:], func=ACT.Sigmoid, bias=bias_col[:, j : j + 1], scale=1.0
             )
-            if n == PAIR - 1:
-                nc.gpsimd.tensor_tensor(out=result[:], in0=result[:], in1=minus[:], op=ALU.subtract)
-                nc.sync.dma_start(out=out_tiles[:, PAIR * pair : PAIR * (pair + 1), :], in_=result[:])
 
-        for t in range(-TURN_AHEAD, TILES):
-            g, run = divmod(t + GATE_RUNS + 1, GROUP_TILES)
-            if run < GATE_RUNS:
-                gate_run(g, run)
-            blend(t)
-            part = t + TURN_AHEAD
+        def blend(unit):
+            g, j = divmod(unit, CHUNKS)
+            cols = slice(P * j, P * (j + 1))
+            z = z_pool.tile([P, GROUP_TILES, P], F32, name="z", tag="z")
+            for i in range(GROUP_TILES):
+                nc.tensor.transpose(z[:, i, :], gate_tiles[unit][:, P * i : P * (i + 1)], ident[:])
+            plus = blend_pool.tile([P, GROUP_TILES, P], F32, name="plus", tag="plus")
+            minus = blend_pool.tile([P, GROUP_TILES, P], F32, name="minus", tag="minus")
+            nc.vector.tensor_tensor(out=plus[:], in0=z[:], in1=sources[(STATE, g)][:, :, cols], op=ALU.mult)
+            nc.vector.scalar_tensor_tensor(
+                out=minus[:], in0=z[:], scalar=1.0, in1=sources[("c", g)][:, :, cols], op0=ALU.subtract, op1=ALU.mult
+            )
+            rows = slice(GROUP_TILES * g, GROUP_TILES * (g + 1))
+            if g < GROUPS - 1:
+                if j == 0:
+                    result_tiles[g] = result_pool.tile([P, GROUP_TILES, FEATURES], F32, name="result", tag="result")
+                nc.gpsimd.tensor_tensor(out=result_tiles[g][:, :, cols], in0=plus[:], in1=minus[:], op=ALU.subtract)
+                if j == CHUNKS - 1:
+                    nc.sync.dma_start(out=out_tiles[:, rows, :], in_=result_tiles[g][:])
+            else:
+                last = last_pool.tile([P, GROUP_TILES, P], F32, name="last", tag="last")
+                engine = nc.vector if unit == UNITS - 1 else nc.gpsimd
+                engine.tensor_tensor(out=last[:], in0=plus[:], in1=minus[:], op=ALU.subtract)
+                nc.sync.dma_start(out=out_tiles[:, rows, cols], in_=last[:])
+
+        waiting = []
+
+        def quantise_waiting():
+            for g, operand in waiting:
+                quantise(g, operand)
+            waiting.clear()
+
+        def turn_in_next(part):
             turn_in(part)
-            if part < PARTS and part % GROUP_PARTS == GROUP_PARTS - 1:
-                quantise(part // GROUP_PARTS)
+            if part % 2 == 1:
+                waiting.append((part // GROUP_PARTS, (part % GROUP_PARTS) // 2))
+
+        for part in range(HEAD_PARTS):
+            quantise_waiting()
+            turn_in_next(part)
+            if part == 1:
+                nc.vector.tensor_copy(out=bias_rows_f32[:], in_=bias_rows[:])
+                bias_turned = turned_pool.tile([P, 2, PART_TILES * P], F32, name="bias_turned", tag="turned")
+                nc.tensor.transpose(bias_turned[:, 0, 0:P], bias_rows_f32[:], ident[:])
+                nc.vector.tensor_copy(out=bias_col[:], in_=bias_turned[:, 0, 0:CHUNKS])
+        quantise_waiting()
+        for unit in range(RUN_UNITS):
+            gate(unit)
+        turned_in = HEAD_PARTS
+        for unit in range(UNITS):
+            blend(unit)
+            if unit % RUN_UNITS == 0:
+                for ahead in range(RUN_UNITS):
+                    gate(unit + RUN_UNITS + ahead)
+            quantise_waiting()
+            goal = min(PARTS, unit + 1 + TURN_AHEAD, turned_in + CATCH_UP)
+            while turned_in < goal:
+                turn_in_next(turned_in)
+                turned_in += 1

@@ -30,10 +30,11 @@ PART_TILES = 2
 GROUP_PARTS = 2 * GROUP_TILES // PART_TILES
 PARTS = GROUPS * GROUP_PARTS
 HEAD_PARTS = 6
-TURN_AHEAD = 10
+TURN_AHEAD = 8
 CATCH_UP = 2
 RUN_UNITS = 2
 SPLIT_GROUPS = 2
+VECTOR_ENDS = 2
 
 FLOPS = 2 * 2 * ROWS * FEATURES * FEATURES
 
@@ -187,7 +188,7 @@ def tile_grulrcell_pb_t_kernel(
                     nc.sync.dma_start(out=out_tiles[:, rows, :], in_=result_tiles[g][:])
             else:
                 last = last_pool.tile([P, GROUP_TILES, P], F32, name="last", tag="last")
-                engine = nc.vector if unit == UNITS - 1 else nc.gpsimd
+                engine = nc.vector if unit >= UNITS - VECTOR_ENDS else nc.gpsimd
                 engine.tensor_tensor(out=last[:], in0=plus[:], in1=minus[:], op=ALU.subtract)
                 nc.sync.dma_start(out=out_tiles[:, rows, cols], in_=last[:])
 

@@ -101,12 +101,12 @@ def tile_grulrcell_pb_t_kernel(
                         in_=scales[0, 4 * quadrant : 4 * quadrant + 4, :].bitcast(I32),
                     )
 
-        nc.sync.dma_start(out=bias_rows[0:CHUNKS, :], in_=bias_gate.rearrange("o (j m) -> (o j) m", j=CHUNKS))
         for g in range(GROUPS):
             pieces = 2 if g < SPLIT_GROUPS else 1
             sources[(INPUT, g)], moves = load(inp_tiles, "inp", g, pieces)
             start(moves)
             if g == 1:
+                nc.sync.dma_start(out=bias_rows[0:CHUNKS, :], in_=bias_gate.rearrange("o (j m) -> (o j) m", j=CHUNKS))
                 load_weights()
             sources[(STATE, g)], moves = load(state_tiles, "state", g, pieces)
             start(moves)
@@ -207,7 +207,7 @@ def tile_grulrcell_pb_t_kernel(
         for part in range(HEAD_PARTS):
             quantise_waiting()
             turn_in_next(part)
-            if part == 1:
+            if part == HEAD_PARTS - 1:
                 nc.vector.tensor_copy(out=bias_rows_f32[:], in_=bias_rows[:])
                 bias_turned = turned_pool.tile([P, 2, PART_TILES * P], F32, name="bias_turned", tag="turned")
                 nc.tensor.transpose(bias_turned[:, 0, 0:P], bias_rows_f32[:], ident[:])

@@ -61,7 +61,6 @@ def tile_grulrcell_pb_t_kernel(
         turned_pool = stack.enter_context(tc.psum_pool(name="turned", bufs=3))
         sum_pool = stack.enter_context(tc.psum_pool(name="sums", bufs=2))
         z_pool = stack.enter_context(tc.psum_pool(name="z", bufs=3))
-        stack.enter_context(tc.manual_schedule())
 
         weight_words = const.tile([P, 2, 2 * FEATURES], U8, align_bytes=64)
         weight_planes = const.tile([P, 2, FEATURES], U8, align_bytes=64)

@@ -217,9 +217,7 @@ def tile_grulrcell_pb_t_kernel(
         turned_in = HEAD_PARTS
         for unit in range(UNITS):
             blend(unit)
-            if unit % RUN_UNITS == 0:
-                for ahead in range(RUN_UNITS):
-                    gate(unit + RUN_UNITS + ahead)
+            gate(unit + RUN_UNITS)
             quantise_waiting()
             goal = min(PARTS, unit + 1 + TURN_AHEAD, turned_in + CATCH_UP)
             while turned_in < goal:

@@ -29,12 +29,15 @@ STATE = 1
 PART_TILES = 2
 GROUP_PARTS = 2 * GROUP_TILES // PART_TILES
 PARTS = GROUPS * GROUP_PARTS
-HEAD_PARTS = 6
+FINE_GROUPS = 1
+FINE_EXTRA = FINE_GROUPS * GROUP_PARTS
+HEAD_PARTS = 6 + FINE_EXTRA
 TURN_AHEAD = 8
 CATCH_UP = 2
 RUN_UNITS = 2
 SPLIT_GROUPS = 2
-VECTOR_ENDS = 2
+TENSOR_GROUPS = (7,)
+VECTOR_ENDS = 3
 
 FLOPS = 2 * 2 * ROWS * FEATURES * FEATURES
 
@@ -58,6 +61,7 @@ def tile_grulrcell_pb_t_kernel(
         blend_pool = stack.enter_context(tc.tile_pool(name="blend", bufs=4))
         result_pool = stack.enter_context(tc.tile_pool(name="result", bufs=GROUPS - 1))
         last_pool = stack.enter_context(tc.tile_pool(name="last", bufs=CHUNKS))
+        gap_pool = stack.enter_context(tc.tile_pool(name="gap", bufs=1))
         turned_pool = stack.enter_context(tc.psum_pool(name="turned", bufs=3))
         sum_pool = stack.enter_context(tc.psum_pool(name="sums", bufs=2))
         z_pool = stack.enter_context(tc.psum_pool(name="z", bufs=3))
@@ -75,6 +79,10 @@ def tile_grulrcell_pb_t_kernel(
         nc.vector.memset(table_warmer[:], 0.0)
         nc.scalar.activation(out=table_warmer[:, 1:2], in_=table_warmer[:, 0:1], func=ACT.Sigmoid)
         make_identity(nc, ident[:])
+        plus_one = const.tile([P, P], BF16)
+        minus_one = const.tile([P, P], BF16)
+        nc.vector.tensor_copy(out=plus_one[:], in_=ident[:])
+        nc.vector.tensor_scalar(out=minus_one[:], in0=ident[:], scalar1=-1.0, scalar2=None, op0=ALU.mult)
 
         sources = {}
 
@@ -101,7 +109,7 @@ def tile_grulrcell_pb_t_kernel(
                     )
 
         for g in range(GROUPS):
-            pieces = 2 if g < SPLIT_GROUPS else 1
+            pieces = 4 if g < FINE_GROUPS else 2 if g < SPLIT_GROUPS else 1
             sources[(INPUT, g)], moves = load(inp_tiles, "inp", g, pieces)
             start(moves)
             if g == 1:
@@ -117,23 +125,29 @@ def tile_grulrcell_pb_t_kernel(
 
         grouped_tiles, code_tiles, plane_tiles, gate_tiles, z_tiles, result_tiles = {}, {}, {}, {}, {}, {}
 
+        part_list = []
+        for g in range(GROUPS):
+            tiles = 1 if g < FINE_GROUPS else PART_TILES
+            for operand in (INPUT, STATE):
+                for first in range(0, GROUP_TILES, tiles):
+                    part_list.append((g, operand, first, tiles))
+
         def turn_in(part):
-            g, q = divmod(part, GROUP_PARTS)
-            operand, half = divmod(q, 2)
-            if half == 0:
+            g, operand, first, tiles = part_list[part]
+            if first == 0:
                 grouped_tiles[(g, operand)] = grouped_pool.tile(
                     [P, GROUP_ROWS, PACK], BF16, name="grouped", tag="grouped", align_bytes=64
                 )
             source = sources[(operand, g)]
             turned = turned_pool.tile([P, 2, PART_TILES * P], F32, name="turned", tag="turned")
-            for n in range(PART_TILES):
-                words = source[:, PART_TILES * half + n, :].bitcast(F32)
+            for n in range(tiles):
+                words = source[:, first + n, :].bitcast(F32)
                 for u in range(2):
                     nc.tensor.transpose(turned[:, u, P * n : P * (n + 1)], words[:, u:WORDS:2], ident[:])
-            rows = slice(PART_TILES * P * half, PART_TILES * P * (half + 1))
+            rows = slice(P * first, P * (first + tiles))
             nc.scalar.copy(
                 out=grouped_tiles[(g, operand)][:, rows, :].bitcast(F32),
-                in_=turned[:].rearrange("p u r -> p r u"),
+                in_=turned[:, :, 0 : P * tiles].rearrange("p u r -> p r u"),
             )
 
         def quantise(g, operand):
@@ -166,6 +180,17 @@ def tile_grulrcell_pb_t_kernel(
                 out=gate_tiles[unit][:], in_=sums[:], func=ACT.Sigmoid, bias=bias_col[:, j : j + 1], scale=1.0
             )
 
+        gap_tiles = {}
+
+        def gap(g, i):
+            if i == 0:
+                gap_tiles[g] = gap_pool.tile([P, GROUP_TILES, FEATURES], F32, name="gap", tag="gap")
+            bank = turned_pool.tile([P, 2, PART_TILES * P], F32, name="gap_bank", tag="turned")
+            flat = bank[:].rearrange("p u r -> p (u r)")
+            nc.tensor.matmul(out=flat, lhsT=plus_one[:], rhs=sources[(STATE, g)][:, i, :], start=True, stop=False)
+            nc.tensor.matmul(out=flat, lhsT=minus_one[:], rhs=sources[("c", g)][:, i, :], start=False, stop=True)
+            nc.scalar.copy(out=gap_tiles[g][:, i, :], in_=flat)
+
         def blend(unit):
             g, j = divmod(unit, CHUNKS)
             cols = slice(P * j, P * (j + 1))
@@ -173,23 +198,34 @@ def tile_grulrcell_pb_t_kernel(
             for i in range(GROUP_TILES):
                 nc.tensor.transpose(z[:, i, :], gate_tiles[unit][:, P * i : P * (i + 1)], ident[:])
             plus = blend_pool.tile([P, GROUP_TILES, P], F32, name="plus", tag="plus")
-            minus = blend_pool.tile([P, GROUP_TILES, P], F32, name="minus", tag="minus")
-            nc.vector.tensor_tensor(out=plus[:], in0=z[:], in1=sources[(STATE, g)][:, :, cols], op=ALU.mult)
-            nc.vector.scalar_tensor_tensor(
-                out=minus[:], in0=z[:], scalar=1.0, in1=sources[("c", g)][:, :, cols], op0=ALU.subtract, op1=ALU.mult
-            )
+            if g in TENSOR_GROUPS:
+                nc.vector.tensor_tensor(out=plus[:], in0=z[:], in1=gap_tiles[g][:, :, cols], op=ALU.mult)
+                other, last_op = sources[("c", g)][:, :, cols], ALU.add
+            else:
+                minus = blend_pool.tile([P, GROUP_TILES, P], F32, name="minus", tag="minus")
+                nc.vector.tensor_tensor(out=plus[:], in0=z[:], in1=sources[(STATE, g)][:, :, cols], op=ALU.mult)
+                nc.vector.scalar_tensor_tensor(
+                    out=minus[:], in0=z[:], scalar=1.0, in1=sources[("c", g)][:, :, cols], op0=ALU.subtract, op1=ALU.mult
+                )
+                other, last_op = minus[:], ALU.subtract
             rows = slice(GROUP_TILES * g, GROUP_TILES * (g + 1))
             if g < GROUPS - 1:
                 if j == 0:
                     result_tiles[g] = result_pool.tile([P, GROUP_TILES, FEATURES], F32, name="result", tag="result")
-                nc.gpsimd.tensor_tensor(out=result_tiles[g][:, :, cols], in0=plus[:], in1=minus[:], op=ALU.subtract)
+                nc.gpsimd.tensor_tensor(out=result_tiles[g][:, :, cols], in0=plus[:], in1=other, op=last_op)
                 if j == CHUNKS - 1:
                     nc.sync.dma_start(out=out_tiles[:, rows, :], in_=result_tiles[g][:])
             else:
                 last = last_pool.tile([P, GROUP_TILES, P], F32, name="last", tag="last")
                 engine = nc.vector if unit >= UNITS - VECTOR_ENDS else nc.gpsimd
-                engine.tensor_tensor(out=last[:], in0=plus[:], in1=minus[:], op=ALU.subtract)
-                nc.sync.dma_start(out=out_tiles[:, rows, cols], in_=last[:])
+                pieces = 2 if unit == UNITS - 1 else 1
+                n = GROUP_TILES // pieces
+                for i in range(pieces):
+                    these = slice(n * i, n * (i + 1))
+                    engine.tensor_tensor(out=last[:, these, :], in0=plus[:, these, :], in1=other[:, these, :], op=last_op)
+                    nc.sync.dma_start(
+                        out=out_tiles[:, GROUP_TILES * g + n * i : GROUP_TILES * g + n * (i + 1), cols], in_=last[:, these, :]
+                    )
 
         waiting = []
 
@@ -200,8 +236,9 @@ def tile_grulrcell_pb_t_kernel(
 
         def turn_in_next(part):
             turn_in(part)
-            if part % 2 == 1:
-                waiting.append((part // GROUP_PARTS, (part % GROUP_PARTS) // 2))
+            g, operand, first, tiles = part_list[part]
+            if first + tiles == GROUP_TILES:
+                waiting.append((g, operand))
 
         for part in range(HEAD_PARTS):
             quantise_waiting()
@@ -218,8 +255,10 @@ def tile_grulrcell_pb_t_kernel(
         for unit in range(UNITS):
             blend(unit)
             gate(unit + RUN_UNITS)
+            if unit // CHUNKS + 1 in TENSOR_GROUPS:
+                gap(unit // CHUNKS + 1, unit % CHUNKS)
             quantise_waiting()
-            goal = min(PARTS, unit + 1 + TURN_AHEAD, turned_in + CATCH_UP)
+            goal = min(PARTS + FINE_EXTRA, unit + 1 + TURN_AHEAD + FINE_EXTRA, turned_in + CATCH_UP)
             while turned_in < goal:
                 turn_in_next(turned_in)
                 turned_in += 1

from contextlib import ExitStack

import concourse.mybir as mybir
from concourse.masks import make_identity

F32 = mybir.dt.float32
BF16 = mybir.dt.bfloat16
I32 = mybir.dt.int32
U32 = mybir.dt.uint32
U8 = mybir.dt.uint8
FP8X4 = mybir.dt.float8_e4m3fn_x4
FP4X4 = mybir.dt.float4_e2m1fn_x4
ALU = mybir.AluOpType
ACT = mybir.ActivationFunctionType

P = 128
PACK = 4
ROWS = 4096
FEATURES = P * PACK
TILES = ROWS // P
GROUP_TILES = 4
GROUP_ROWS = GROUP_TILES * P
GROUPS = TILES // GROUP_TILES
CHUNKS = FEATURES // P
UNITS = GROUPS * CHUNKS
WORDS = FEATURES // 2
INPUT = 0
STATE = 1
PART_TILES = 2
GROUP_PARTS = 2 * GROUP_TILES // PART_TILES
PARTS = GROUPS * GROUP_PARTS
FINE_GROUPS = 1
FINE_EXTRA = FINE_GROUPS * GROUP_PARTS
HEAD_PARTS = 6 + FINE_EXTRA
TURN_AHEAD = 8
CATCH_UP = 2
RUN_UNITS = 2
SPLIT_GROUPS = 2
TENSOR_GROUPS = (7,)
VECTOR_ENDS = 3

FLOPS = 2 * 2 * ROWS * FEATURES * FEATURES


def tile_grulrcell_pb_t_kernel(
    tc, inp, state, cand, w2_words, w2_scales, u2_words, u2_scales, bias_gate, out
):
    nc = tc.nc
    by_tile = "(p t) f -> p t f"
    inp_tiles = inp.rearrange(by_tile, t=TILES)
    state_tiles = state.rearrange(by_tile, t=TILES)
    cand_tiles = cand.rearrange(by_tile, t=TILES)
    out_tiles = out.rearrange(by_tile, t=TILES)

    with ExitStack() as stack:
        const = stack.enter_context(tc.tile_pool(name="const", bufs=1))
        resident = stack.enter_context(tc.tile_pool(name="resident", bufs=GROUPS))
        grouped_pool = stack.enter_context(tc.tile_pool(name="grouped", bufs=4))
        mx_pool = stack.enter_context(tc.tile_pool(name="mx", bufs=6))
        gate_pool = stack.enter_context(tc.tile_pool(name="gate", bufs=4))
        blend_pool = stack.enter_context(tc.tile_pool(name="blend", bufs=4))
        result_pool = stack.enter_context(tc.tile_pool(name="result", bufs=GROUPS - 1))
        last_pool = stack.enter_context(tc.tile_pool(name="last", bufs=CHUNKS))
        gap_pool = stack.enter_context(tc.tile_pool(name="gap", bufs=1))
        turned_pool = stack.enter_context(tc.psum_pool(name="turned", bufs=3))
        sum_pool = stack.enter_context(tc.psum_pool(name="sums", bufs=2))
        z_pool = stack.enter_context(tc.psum_pool(name="z", bufs=3))

        weight_words = const.tile([P, 2, 2 * FEATURES], U8, align_bytes=64)
        weight_planes = const.tile([P, 2, FEATURES], U8, align_bytes=64)
        bias_rows = const.tile([P, P], BF16)
        bias_rows_f32 = const.tile([P, P], F32)
        bias_col = const.tile([P, CHUNKS], F32)
        ident = const.tile([P, P], F32)
        table_warmer = const.tile([P, 2], F32)

        nc.vector.memset(bias_rows[:], 0.0)
        nc.vector.memset(weight_planes[:].bitcast(I32), 0)
        nc.vector.memset(table_warmer[:], 0.0)
        nc.scalar.activation(out=table_warmer[:, 1:2], in_=table_warmer[:, 0:1], func=ACT.Sigmoid)
        make_identity(nc, ident[:])
        plus_one = const.tile([P, P], BF16)
        minus_one = const.tile([P, P], BF16)
        nc.vector.tensor_copy(out=plus_one[:], in_=ident[:])
        nc.vector.tensor_scalar(out=minus_one[:], in0=ident[:], scalar1=-1.0, scalar2=None, op0=ALU.mult)

        sources = {}

        def load(dram_tiles, tag, g, pieces):
            t = resident.tile([P, GROUP_TILES, FEATURES], BF16, name=tag, tag=tag)
            n = GROUP_TILES // pieces
            return t, [
                (t[:, n * i : n * (i + 1), :], dram_tiles[:, GROUP_TILES * g + n * i : GROUP_TILES * g + n * (i + 1), :])
                for i in range(pieces)
            ]

        def start(moves):
            for dst, src in moves:
                nc.sync.dma_start(out=dst, in_=src)

        def load_weights():
            for operand, words in ((INPUT, w2_words), (STATE, u2_words)):
                nc.sync.dma_start(out=weight_words[:, operand, :].bitcast(I32), in_=words[0].bitcast(I32))
            for operand, scales in ((INPUT, w2_scales), (STATE, u2_scales)):
                for quadrant in range(4):
                    nc.sync.dma_start(
                        out=weight_planes[32 * quadrant : 32 * quadrant + 4, operand, :].bitcast(I32),
                        in_=scales[0, 4 * quadrant : 4 * quadrant + 4, :].bitcast(I32),
                    )

        for g in range(GROUPS):
            pieces = 4 if g < FINE_GROUPS else 2 if g < SPLIT_GROUPS else 1
            sources[(INPUT, g)], moves = load(inp_tiles, "inp", g, pieces)
            start(moves)
            if g == 1:
                nc.sync.dma_start(out=bias_rows[0:CHUNKS, :], in_=bias_gate.rearrange("o (j m) -> (o j) m", j=CHUNKS))
                load_weights()
            sources[(STATE, g)], moves = load(state_tiles, "state", g, pieces)
            start(moves)
            if g >= 1:
                sources[("c", g - 1)], moves = load(cand_tiles, "cand", g - 1, 1)
                start(moves)
        sources[("c", GROUPS - 1)], moves = load(cand_tiles, "cand", GROUPS - 1, 1)
        start(moves)

        grouped_tiles, code_tiles, plane_tiles, gate_tiles, z_tiles, result_tiles = {}, {}, {}, {}, {}, {}

        part_list = []
        for g in range(GROUPS):
            tiles = 1 if g < FINE_GROUPS else PART_TILES
            for operand in (INPUT, STATE):
                for first in range(0, GROUP_TILES, tiles):
                    part_list.append((g, operand, first, tiles))

        def turn_in(part):
            g, operand, first, tiles = part_list[part]
            if first == 0:
                grouped_tiles[(g, operand)] = grouped_pool.tile(
                    [P, GROUP_ROWS, PACK], BF16, name="grouped", tag="grouped", align_bytes=64
                )
            source = sources[(operand, g)]
            turned = turned_pool.tile([P, 2, PART_TILES * P], F32, name="turned", tag="turned")
            for n in range(tiles):
                words = source[:, first + n, :].bitcast(F32)
                for u in range(2):
                    nc.tensor.transpose(turned[:, u, P * n : P * (n + 1)], words[:, u:WORDS:2], ident[:])
            rows = slice(P * first, P * (first + tiles))
            nc.scalar.copy(
                out=grouped_tiles[(g, operand)][:, rows, :].bitcast(F32),
                in_=turned[:, :, 0 : P * tiles].rearrange("p u r -> p r u"),
            )

        def quantise(g, operand):
            key = (g, operand)
            code_tiles[key] = mx_pool.tile([P, GROUP_ROWS], U32, name="codes", tag="codes", align_bytes=64)
            plane_tiles[key] = mx_pool.tile([P, GROUP_ROWS], U8, name="planes", tag="planes", align_bytes=64)
            nc.vector.quantize_mx(
                out=code_tiles[key][:].bitcast(FP8X4),
                scales=plane_tiles[key][:],
                in_=grouped_tiles[key][:].rearrange("p r j -> p (r j)"),
            )

        def gate(unit):
            if unit >= UNITS:
                return
            g, j = divmod(unit, CHUNKS)
            sums = sum_pool.tile([P, GROUP_ROWS], F32, name="sums", tag="sums")
            for operand in (INPUT, STATE):
                nc.tensor.matmul_mx(
                    out=sums[:],
                    lhsT=weight_words[:, operand, 2 * P * j : 2 * P * (j + 1)].bitcast(FP4X4),
                    lhsT_scale=weight_planes[:, operand, P * j : P * (j + 1)],
                    rhs=code_tiles[(g, operand)][:].bitcast(FP8X4),
                    rhs_scale=plane_tiles[(g, operand)][:],
                    start=(operand == INPUT),
                    stop=(operand == STATE),
                )
            gate_tiles[unit] = gate_pool.tile([P, GROUP_ROWS], F32, name="gate", tag="gate")
            nc.scalar.activation(
                out=gate_tiles[unit][:], in_=sums[:], func=ACT.Sigmoid, bias=bias_col[:, j : j + 1], scale=1.0
            )

        gap_tiles = {}

        def gap(g, i):
            if i == 0:
                gap_tiles[g] = gap_pool.tile([P, GROUP_TILES, FEATURES], F32, name="gap", tag="gap")
            bank = turned_pool.tile([P, 2, PART_TILES * P], F32, name="gap_bank", tag="turned")
            flat = bank[:].rearrange("p u r -> p (u r)")
            nc.tensor.matmul(out=flat, lhsT=plus_one[:], rhs=sources[(STATE, g)][:, i, :], start=True, stop=False)
            nc.tensor.matmul(out=flat, lhsT=minus_one[:], rhs=sources[("c", g)][:, i, :], start=False, stop=True)
            nc.scalar.copy(out=gap_tiles[g][:, i, :], in_=flat)

        def blend(unit):
            g, j = divmod(unit, CHUNKS)
            cols = slice(P * j, P * (j + 1))
            z = z_pool.tile([P, GROUP_TILES, P], F32, name="z", tag="z")
            for i in range(GROUP_TILES):
                nc.tensor.transpose(z[:, i, :], gate_tiles[unit][:, P * i : P * (i + 1)], ident[:])
            plus = blend_pool.tile([P, GROUP_TILES, P], F32, name="plus", tag="plus")
            if g in TENSOR_GROUPS:
                nc.vector.tensor_tensor(out=plus[:], in0=z[:], in1=gap_tiles[g][:, :, cols], op=ALU.mult)
                other, last_op = sources[("c", g)][:, :, cols], ALU.add
            else:
                minus = blend_pool.tile([P, GROUP_TILES, P], F32, name="minus", tag="minus")
                nc.vector.tensor_tensor(out=plus[:], in0=z[:], in1=sources[(STATE, g)][:, :, cols], op=ALU.mult)
                nc.vector.scalar_tensor_tensor(
                    out=minus[:], in0=z[:], scalar=1.0, in1=sources[("c", g)][:, :, cols], op0=ALU.subtract, op1=ALU.mult
                )
                other, last_op = minus[:], ALU.subtract
            rows = slice(GROUP_TILES * g, GROUP_TILES * (g + 1))
            if g < GROUPS - 1:
                if j == 0:
                    result_tiles[g] = result_pool.tile([P, GROUP_TILES, FEATURES], F32, name="result", tag="result")
                nc.gpsimd.tensor_tensor(out=result_tiles[g][:, :, cols], in0=plus[:], in1=other, op=last_op)
                if j == CHUNKS - 1:
                    nc.sync.dma_start(out=out_tiles[:, rows, :], in_=result_tiles[g][:])
            else:
                last = last_pool.tile([P, GROUP_TILES, P], F32, name="last", tag="last")
                engine = nc.vector if unit >= UNITS - VECTOR_ENDS else nc.gpsimd
                pieces = 2 if unit == UNITS - 1 else 1
                n = GROUP_TILES // pieces
                for i in range(pieces):
                    these = slice(n * i, n * (i + 1))
                    engine.tensor_tensor(out=last[:, these, :], in0=plus[:, these, :], in1=other[:, these, :], op=last_op)
                    nc.sync.dma_start(
                        out=out_tiles[:, GROUP_TILES * g + n * i : GROUP_TILES * g + n * (i + 1), cols], in_=last[:, these, :]
                    )

        waiting = []

        def quantise_waiting():
            for g, operand in waiting:
                quantise(g, operand)
            waiting.clear()

        def turn_in_next(part):
            turn_in(part)
            g, operand, first, tiles = part_list[part]
            if first + tiles == GROUP_TILES:
                waiting.append((g, operand))

        for part in range(HEAD_PARTS):
            quantise_waiting()
            turn_in_next(part)
            if part == HEAD_PARTS - 1:
                nc.vector.tensor_copy(out=bias_rows_f32[:], in_=bias_rows[:])
                bias_turned = turned_pool.tile([P, 2, PART_TILES * P], F32, name="bias_turned", tag="turned")
                nc.tensor.transpose(bias_turned[:, 0, 0:P], bias_rows_f32[:], ident[:])
                nc.vector.tensor_copy(out=bias_col[:], in_=bias_turned[:, 0, 0:CHUNKS])
        quantise_waiting()
        for unit in range(RUN_UNITS):
            gate(unit)
        turned_in = HEAD_PARTS
        for unit in range(UNITS):
            blend(unit)
            gate(unit + RUN_UNITS)
            if unit // CHUNKS + 1 in TENSOR_GROUPS:
                gap(unit // CHUNKS + 1, unit % CHUNKS)
            quantise_waiting()
            goal = min(PARTS + FINE_EXTRA, unit + 1 + TURN_AHEAD + FINE_EXTRA, turned_in + CATCH_UP)
            while turned_in < goal:
                turn_in_next(turned_in)
                turned_in += 1
